import numpy as np
import ml_dtypes


def mxq(x, axis, fmt="e4m3"):
    dtype, down = {"e4m3": (ml_dtypes.float8_e4m3fn, 7), "e5m2": (ml_dtypes.float8_e5m2, 14)}[fmt]
    v = np.moveaxis(np.asarray(x, np.float32).astype(ml_dtypes.bfloat16).astype(np.float64), axis, -1)
    blocks = v.reshape(v.shape[:-1] + (-1, 32))
    amax = np.abs(blocks).max(-1, keepdims=True)
    byte = np.maximum(np.where(amax > 0, np.frexp(amax)[1] - 1 + 127, 0) - down, 1)
    scale = np.exp2(byte - 127.0)
    codes = (blocks / scale).astype(np.float32).astype(dtype).astype(np.float64)
    return np.moveaxis((codes * scale).reshape(v.shape), -1, axis)


WIDE = False


def mx_kscale(k):
    if not WIDE:
        return np.ones(k)
    levels = np.array([10, -10, 5, -5, 0])
    a = np.random.permutation(np.resize(levels, k // 512 * 4)).reshape(k // 512, 4)
    idx = np.arange(k)
    return np.exp2(a[idx // 512, idx % 128 // 32])


BF16 = ml_dtypes.bfloat16


def bf(x):
    return np.asarray(x, np.float32).astype(BF16)


def f64(x):
    return np.asarray(x).astype(np.float64)


B, S, D, H, F = 4, 256, 1024, 16, 4096
EPS = 1e-5
NTERMS = 120


def layernorm(v, gamma, beta):
    mu = v.mean(-1, keepdims=True)
    var = np.square(v - mu).mean(-1, keepdims=True)
    return (v - mu) / np.sqrt(var + EPS) * gamma + beta


def erf(z):
    z = np.clip(z, -6.0, 6.0)
    zz = 2.0 * z * z
    term = z.copy()
    tot = z.copy()
    for n in range(1, NTERMS):
        term *= zz
        term /= 2.0 * n + 1.0
        tot += term
    return 2.0 / np.sqrt(np.pi) * np.exp(-z * z) * tot


def gelu(v):
    return 0.5 * v * (1.0 + erf(v / np.sqrt(2.0)))


def setup_inputs():
    s, t = mx_kscale(D), mx_kscale(D)
    return {"attn_out": bf(0.25 * np.random.standard_normal((B, S, D)) * s),
            "x": bf(np.random.standard_normal((B, S, D)) * (0.5 + np.random.random((B, S, 1))) + 0.5 * np.random.standard_normal((B, S, 1))),
            "w_proj": bf(2.0 * np.random.standard_normal((D, D)) / np.sqrt(D) / s[:, None]),
            "b_proj": bf(0.1 * np.random.standard_normal(D)),
            "g2": bf((1.0 + 0.1 * np.random.standard_normal(D)) * t),
            "beta2": bf(0.1 * np.random.standard_normal(D) * t),
            "w_fc1": bf(np.random.standard_normal((D, F)) / np.sqrt(D) / t[:, None]),
            "b_fc1": bf(0.1 * np.random.standard_normal(F))}


def reference(attn_out, x, w_proj, b_proj, g2, beta2, w_fc1, b_fc1):
    x_mid = f64(x) + ((mxq(f64(attn_out), 2, "e4m3") @ mxq(f64(w_proj), 0, "e4m3")) + f64(b_proj))
    h = layernorm(x_mid, f64(g2), f64(beta2))
    hid = gelu((mxq(h, 2, "e4m3") @ mxq(f64(w_fc1), 0, "e4m3")) + f64(b_fc1))
    return x_mid, hid

@@ -1,0 +1,317 @@
+from contextlib import ExitStack
+
+import concourse.mybir as mybir
+from concourse.masks import make_identity
+
+F32 = mybir.dt.float32
+BF16 = mybir.dt.bfloat16
+U32 = mybir.dt.uint32
+U8 = mybir.dt.uint8
+FP8X4 = mybir.dt.float8_e4m3fn_x4
+ALU = mybir.AluOpType
+ACT = mybir.ActivationFunctionType
+
+P = 128
+PACK = 4
+K_PASS = P * PACK
+TOKENS = 1024
+D = 1024
+F = 4096
+EPS = 1e-5
+PASSES = D // K_PASS
+TILES = TOKENS // P
+GROUP = 4
+GROUPS = TILES // GROUP
+BANK = 512
+PIECE = 1024
+F_PIECES = F // PIECE
+SLABS = D // P
+VECTOR_COLS = 512
+W_BUFS = 4
+X_MID_BUFS = 5
+HID_BUFS = 6
+
+FLOPS = 2 * TOKENS * D * D + 2 * TOKENS * D * F
+
+
+def tile_flashinferblock_pb_kernel(
+    tc, attn_out, x, w_proj, b_proj, g2, beta2, w_fc1, b_fc1, out_0, out_1
+):
+    nc = tc.nc
+    with ExitStack() as ctx:
+        const = ctx.enter_context(tc.tile_pool(name="const", bufs=1))
+        keep = ctx.enter_context(tc.tile_pool(name="keep", bufs=1))
+        loads = ctx.enter_context(tc.tile_pool(name="loads", bufs=TILES))
+        stage = ctx.enter_context(tc.tile_pool(name="stage", bufs=2))
+        rows = ctx.enter_context(tc.tile_pool(name="rows", bufs=GROUP))
+        tp_psum = ctx.enter_context(tc.psum_pool(name="tp_psum", bufs=3))
+        acc_psum = ctx.enter_context(tc.psum_pool(name="acc_psum", bufs=5))
+
+        attn_v = attn_out.flatten_outer_dims().rearrange("(p i) k -> p i k", i=TILES)
+        x_v = x.flatten_outer_dims().rearrange("(p i) d -> p i d", i=TILES)
+        x_mid_v = out_0.flatten_outer_dims().rearrange("(p i) d -> p i d", i=TILES)
+        hid_v = out_1.flatten_outer_dims().rearrange("(p i) f -> p i f", i=TILES)
+
+        warm = const.tile([P, 1], F32)
+        nc.vector.memset(warm[:], 0.0)
+        nc.scalar.activation(out=warm[:], in_=warm[:], func=ACT.Gelu)
+
+        ident = const.tile([P, P], F32)
+        make_identity(nc, ident[:])
+        neg_half = const.tile([P, GROUP], F32)
+        nc.vector.memset(neg_half[:], -0.5)
+
+        gb_rows = const.tile([P, P], BF16)
+        nc.vector.memset(gb_rows[:], 0.0)
+        nc.sync.dma_start(out=gb_rows[0:SLABS, :], in_=g2.rearrange("(j p) -> j p", p=P))
+        nc.sync.dma_start(out=gb_rows[SLABS : 2 * SLABS, :], in_=beta2.rearrange("(j p) -> j p", p=P))
+        gb_rows_f32 = const.tile([P, P], F32)
+        nc.vector.tensor_copy(out=gb_rows_f32[:], in_=gb_rows[:])
+        gb_ps = tp_psum.tile([P, GROUP, P], F32, tag="tp")
+        nc.tensor.transpose(gb_ps[:, 0, :], gb_rows_f32[:], ident[:])
+        gain_shift = const.tile([P, 2 * SLABS], F32)
+        nc.vector.tensor_copy(out=gain_shift[:], in_=gb_ps[:, 0, 0 : 2 * SLABS])
+
+        b_proj_all = const.tile([P, D], BF16)
+        b_fc1_all = const.tile([P, F], BF16)
+
+        def load_b_fc1(c):
+            cols = slice(c * PIECE, (c + 1) * PIECE)
+            nc.sync.dma_start(out=b_fc1_all[:, cols], in_=b_fc1[cols].partition_broadcast(P))
+
+        wp_codes = keep.tile([P, PASSES, D], U32, align_bytes=64)
+        wp_scales = keep.tile([P, PASSES, D], U8, align_bytes=64)
+        wf_codes = keep.tile([P, PASSES, F], U32, align_bytes=64)
+        wf_scales = keep.tile([P, PASSES, F], U8, align_bytes=64)
+
+        wp_v = w_proj.rearrange("(g u p e) n -> g p u e n", g=PASSES, u=2, p=P, e=2)
+        wf_v = w_fc1.rearrange("(g t p) n -> g p t n", g=PASSES, t=PACK, p=P)
+        n_pieces = PASSES + PASSES * F_PIECES
+        w_raw = {}
+
+        def load_weight_piece(k):
+            raw = loads.tile([P, PACK, PIECE], BF16, tag="w_raw", bufs=W_BUFS, name="w_raw")
+            if k < PASSES:
+                nc.sync.dma_start(out=raw[:].rearrange("p (u e) n -> p u e n", u=2), in_=wp_v[k])
+            else:
+                c, g = divmod(k - PASSES, PASSES)
+                nc.sync.dma_start(out=raw[:], in_=wf_v[g][:, :, c * PIECE : (c + 1) * PIECE])
+            w_raw[k] = raw
+
+        def quantise_weight_piece(k):
+            if k < PASSES:
+                codes, scales = wp_codes[:, k, :], wp_scales[:, k, :]
+            else:
+                c, g = divmod(k - PASSES, PASSES)
+                cols = slice(c * PIECE, (c + 1) * PIECE)
+                codes, scales = wf_codes[:, g, cols], wf_scales[:, g, cols]
+            grouped = stage.tile([P, PIECE, PACK], BF16, align_bytes=64, tag="w_grouped", name="w_grouped")
+            src = w_raw[k][:].rearrange("p t (c i) -> p c t i", i=4)
+            dst = grouped[:].rearrange("p (c i) t -> p c t i", i=4)
+            split = VECTOR_COLS // 4
+            nc.vector.tensor_copy(out=dst[:, 0:split], in_=src[:, 0:split])
+            nc.scalar.copy(out=dst[:, split:], in_=src[:, split:])
+            nc.vector.quantize_mx(
+                out=codes.bitcast(FP8X4),
+                scales=scales,
+                in_=grouped[:].rearrange("p n t -> p (n t)"),
+            )
+            if k + W_BUFS < n_pieces:
+                load_weight_piece(k + W_BUFS)
+
+        def load_rows(view, i, tag):
+            raw = loads.tile([P, D], BF16, tag=tag, name=tag)
+            nc.sync.dma_start(out=raw[:], in_=view[:, i, :])
+            return raw
+
+        def token_codes():
+            codes = keep.tile([P, GROUP * PASSES * P], U32, align_bytes=64, tag="tok_codes", bufs=GROUPS, name="tok_codes")
+            scales = keep.tile([P, GROUP * PASSES * P], U8, align_bytes=64, tag="tok_scales", bufs=GROUPS, name="tok_scales")
+            return codes, scales
+
+        def quantise_attention(a_raw, codes, scales):
+            words = a_raw[:].bitcast(F32)
+            at_ps = tp_psum.tile([P, PASSES * 2, P], F32, tag="tp")
+            for s in range(PASSES * 2):
+                nc.tensor.transpose(at_ps[:, s, :], words[:, s * P : (s + 1) * P], ident[:])
+            a_grouped = stage.tile([P, PASSES, P, PACK], BF16, align_bytes=64)
+            nc.scalar.copy(
+                out=a_grouped[:].bitcast(F32),
+                in_=at_ps[:].rearrange("p (g u) r -> p g r u", u=2),
+            )
+            nc.vector.quantize_mx(
+                out=codes.bitcast(FP8X4), scales=scales, in_=a_grouped[:].rearrange("p g r t -> p (g r t)")
+            )
+
+        def add_bias_to_residual(x_raw):
+            xm = rows.tile([P, D], F32, tag="x_mid", bufs=X_MID_BUFS, name="x_mid")
+            nc.gpsimd.tensor_tensor(out=xm[:], in0=x_raw[:], in1=b_proj_all[:], op=ALU.add)
+            return xm
+
+        def new_stats():
+            return {
+                "row_sum": rows.tile([P, 2 * GROUP], F32, tag="row_sum", bufs=2, name="row_sum"),
+                "neg_mean": rows.tile([P, GROUP], F32, tag="neg_mean", bufs=2, name="neg_mean"),
+                "sq_sum": rows.tile([P, GROUP], F32, tag="sq_sum", bufs=2, name="sq_sum"),
+                "var_eps": rows.tile([P, GROUP], F32, tag="var_eps", bufs=2, name="var_eps"),
+                "rstd": rows.tile([P, GROUP], F32, tag="rstd", bufs=2, name="rstd"),
+            }
+
+        def project(i, codes, scales, xm, stats):
+            q = i % GROUP
+            for half in range(D // BANK):
+                cols = slice(half * BANK, (half + 1) * BANK)
+                acc = acc_psum.tile([P, BANK], F32, tag="acc")
+                for g in range(PASSES):
+                    toks = slice((q * PASSES + g) * P, (q * PASSES + g + 1) * P)
+                    nc.tensor.matmul_mx(
+                        out=acc[:],
+                        lhsT=codes[:, toks].bitcast(FP8X4),
+                        lhsT_scale=scales[:, toks],
+                        rhs=wp_codes[:, g, cols].bitcast(FP8X4),
+                        rhs_scale=wp_scales[:, g, cols],
+                        start=(g == 0),
+                        stop=(g == PASSES - 1),
+                    )
+                nc.vector.scalar_tensor_tensor(
+                    out=xm[:, cols],
+                    in0=acc[:],
+                    scalar=0.0,
+                    in1=xm[:, cols],
+                    op0=ALU.add,
+                    op1=ALU.add,
+                    accum_out=stats["row_sum"][:, 2 * q + half : 2 * q + half + 1],
+                )
+            nc.sync.dma_start(out=x_mid_v[:, i, :], in_=xm[:])
+            nc.vector.tensor_scalar(
+                out=stats["neg_mean"][:, q : q + 1],
+                in0=stats["row_sum"][:, 2 * q : 2 * q + 1],
+                scalar1=stats["row_sum"][:, 2 * q + 1 : 2 * q + 2],
+                scalar2=-1.0 / D,
+                op0=ALU.add,
+                op1=ALU.mult,
+            )
+            z = rows.tile([P, D], F32, tag="normed", name="normed")
+            nc.scalar.activation(
+                out=z[:],
+                in_=xm[:],
+                func=ACT.Square,
+                bias=stats["neg_mean"][:, q : q + 1],
+                scale=1.0,
+                accum_out=stats["sq_sum"][:, q : q + 1],
+            )
+            return z
+
+        def normalise(x_mid, normed, stats):
+            nc.vector.tensor_scalar(
+                out=stats["var_eps"][:],
+                in0=stats["sq_sum"][:],
+                scalar1=1.0 / D,
+                scalar2=EPS,
+                op0=ALU.mult,
+                op1=ALU.add,
+            )
+            nc.gpsimd.tensor_tensor(out=stats["rstd"][:], in0=stats["var_eps"][:], in1=neg_half[:], op=ALU.pow)
+            for q in range(GROUP):
+                nc.vector.tensor_scalar(
+                    out=normed[q][:],
+                    in0=x_mid[q][:],
+                    scalar1=stats["neg_mean"][:, q : q + 1],
+                    scalar2=stats["rstd"][:, q : q + 1],
+                    op0=ALU.add,
+                    op1=ALU.mult,
+                )
+
+        def quantise_normed(normed, codes, scales):
+            h_slabs = stage.tile([P, SLABS, GROUP * P], BF16, bufs=1)
+            for j in range(SLABS):
+                zt_ps = tp_psum.tile([P, GROUP, P], F32, tag="tp")
+                for q in range(GROUP):
+                    nc.tensor.transpose(zt_ps[:, q, :], normed[q][:, j * P : (j + 1) * P], ident[:])
+                nc.scalar.activation(
+                    out=h_slabs[:, j, :],
+                    in_=zt_ps[:].rearrange("p q r -> p (q r)"),
+                    func=ACT.Identity,
+                    scale=gain_shift[:, j : j + 1],
+                    bias=gain_shift[:, SLABS + j : SLABS + j + 1],
+                )
+            h_grouped = []
+            for g in range(PASSES):
+                hg = stage.tile([P, GROUP * P, PACK], BF16, align_bytes=64, tag="h_grouped", name="h_grouped")
+                nc.vector.tensor_copy(
+                    out=hg[:].rearrange("p (c i) t -> p c t i", i=4),
+                    in_=h_slabs[:, g * PACK : (g + 1) * PACK, :].rearrange("p t (c i) -> p c t i", i=4),
+                )
+                h_grouped.append(hg)
+            for g in range(PASSES):
+                toks = slice(g * GROUP * P, (g + 1) * GROUP * P)
+                nc.vector.quantize_mx(
+                    out=codes[:, toks].bitcast(FP8X4),
+                    scales=scales[:, toks],
+                    in_=h_grouped[g][:].rearrange("p r t -> p (r t)"),
+                )
+
+        def mlp(c, i, codes, scales):
+            q = i % GROUP
+            hid = rows.tile([P, PIECE], F32, tag="hid", bufs=HID_BUFS, name="hid")
+            for half in range(PIECE // BANK):
+                cols = slice(c * PIECE + half * BANK, c * PIECE + (half + 1) * BANK)
+                acc = acc_psum.tile([P, BANK], F32, tag="acc")
+                for g in range(PASSES):
+                    toks = slice((g * GROUP + q) * P, (g * GROUP + q + 1) * P)
+                    nc.tensor.matmul_mx(
+                        out=acc[:],
+                        lhsT=codes[:, toks].bitcast(FP8X4),
+                        lhsT_scale=scales[:, toks],
+                        rhs=wf_codes[:, g, cols].bitcast(FP8X4),
+                        rhs_scale=wf_scales[:, g, cols],
+                        start=(g == 0),
+                        stop=(g == PASSES - 1),
+                    )
+                nc.vector.tensor_tensor(
+                    out=hid[:, half * BANK : (half + 1) * BANK], in0=acc[:], in1=b_fc1_all[:, cols], op=ALU.add
+                )
+            nc.scalar.activation(out=hid[:], in_=hid[:], func=ACT.Gelu)
+            nc.sync.dma_start(out=hid_v[:, i, c * PIECE : (c + 1) * PIECE], in_=hid[:])
+
+        load_weight_piece(0)
+        load_weight_piece(1)
+        a_raw = [load_rows(attn_v, i, "a_raw") for i in range(GROUP)]
+        nc.sync.dma_start(out=b_proj_all[:], in_=b_proj.partition_broadcast(P))
+        x_raw = [load_rows(x_v, i, "x_raw") for i in range(GROUP)]
+        a_raw.extend([load_rows(attn_v, i, "a_raw") for i in range(GROUP, TILES)])
+        x_raw.extend([load_rows(x_v, i, "x_raw") for i in range(GROUP, TILES)])
+        load_weight_piece(2)
+        load_weight_piece(3)
+        load_b_fc1(0)
+
+        quantise_weight_piece(0)
+        quantise_weight_piece(1)
+        a_quant = [token_codes() for grp in range(GROUPS)]
+        for i in range(TILES):
+            codes, scales = a_quant[i // GROUP]
+            cols = slice((i % GROUP) * PASSES * P, (i % GROUP + 1) * PASSES * P)
+            quantise_attention(a_raw[i], codes[:, cols], scales[:, cols])
+        x_mid = [add_bias_to_residual(x_raw[i]) for i in range(X_MID_BUFS)]
+
+        h_quant = []
+        for grp in range(GROUPS):
+            tiles = range(grp * GROUP, (grp + 1) * GROUP)
+            stats = new_stats()
+            codes, scales = a_quant[grp]
+            normed = [project(i, codes, scales, x_mid[i], stats) for i in tiles]
+            normalise([x_mid[i] for i in tiles], normed, stats)
+            if grp == 0:
+                x_mid.extend([add_bias_to_residual(x_raw[i]) for i in range(X_MID_BUFS, TILES)])
+            h_quant.append(token_codes())
+            quantise_normed(normed, h_quant[grp][0], h_quant[grp][1])
+
+        for c in range(1, F_PIECES):
+            load_b_fc1(c)
+        for grp in range(GROUPS):
+            for c in range(F_PIECES):
+                if grp == 0:
+                    for g in range(PASSES):
+                        quantise_weight_piece(PASSES + PASSES * c + g)
+                for i in range(grp * GROUP, (grp + 1) * GROUP):
+                    mlp(c, i, h_quant[grp][0], h_quant[grp][1])

@@ -74,10 +74,18 @@ def tile_flashinferblock_pb_kernel(
 
         b_proj_all = const.tile([P, D], BF16)
         b_fc1_all = const.tile([P, F], BF16)
+        ones = const.tile([P, P], BF16)
+        nc.vector.memset(ones[:], 1.0)
+        bias_row = const.tile([P, PIECE], BF16)
+        nc.vector.memset(bias_row[:], 0.0)
 
-        def load_b_fc1(c):
-            cols = slice(c * PIECE, (c + 1) * PIECE)
-            nc.sync.dma_start(out=b_fc1_all[:, cols], in_=b_fc1[cols].partition_broadcast(P))
+        def spread_bias(bias, spread):
+            nc.sync.dma_start(out=bias_row[0:1, :], in_=bias.rearrange("(o n) -> o n", o=1))
+            spread_ps = tp_psum.tile([P, PIECE], BF16, tag="tp")
+            for half in range(PIECE // BANK):
+                cols = slice(half * BANK, (half + 1) * BANK)
+                nc.tensor.matmul(out=spread_ps[:, cols], lhsT=ones[:], rhs=bias_row[:, cols], start=True, stop=True)
+            nc.scalar.copy(out=spread, in_=spread_ps[:])
 
         wp_codes = keep.tile([P, PASSES, D], U32, align_bytes=64)
         wp_scales = keep.tile([P, PASSES, D], U8, align_bytes=64)
@@ -274,16 +282,15 @@ def tile_flashinferblock_pb_kernel(
             nc.scalar.activation(out=hid[:], in_=hid[:], func=ACT.Gelu)
             nc.sync.dma_start(out=hid_v[:, i, c * PIECE : (c + 1) * PIECE], in_=hid[:])
 
+        spread_bias(b_proj, b_proj_all[:])
         load_weight_piece(0)
         load_weight_piece(1)
         a_raw = [load_rows(attn_v, i, "a_raw") for i in range(GROUP)]
-        nc.sync.dma_start(out=b_proj_all[:], in_=b_proj.partition_broadcast(P))
         x_raw = [load_rows(x_v, i, "x_raw") for i in range(GROUP)]
         a_raw.extend([load_rows(attn_v, i, "a_raw") for i in range(GROUP, TILES)])
         x_raw.extend([load_rows(x_v, i, "x_raw") for i in range(GROUP, TILES)])
         load_weight_piece(2)
         load_weight_piece(3)
-        load_b_fc1(0)
 
         quantise_weight_piece(0)
         quantise_weight_piece(1)
@@ -293,6 +300,8 @@ def tile_flashinferblock_pb_kernel(
             cols = slice((i % GROUP) * PASSES * P, (i % GROUP + 1) * PASSES * P)
             quantise_attention(a_raw[i], codes[:, cols], scales[:, cols])
         x_mid = [add_bias_to_residual(x_raw[i]) for i in range(X_MID_BUFS)]
+        for c in range(F_PIECES):
+            spread_bias(b_fc1[c * PIECE : (c + 1) * PIECE], b_fc1_all[:, c * PIECE : (c + 1) * PIECE])
 
         h_quant = []
         for grp in range(GROUPS):
@@ -306,8 +315,6 @@ def tile_flashinferblock_pb_kernel(
             h_quant.append(token_codes())
             quantise_normed(normed, h_quant[grp][0], h_quant[grp][1])
 
-        for c in range(1, F_PIECES):
-            load_b_fc1(c)
         for grp in range(GROUPS):
             for c in range(F_PIECES):
                 if grp == 0:

@@ -26,9 +26,10 @@ BANK = 512
 PIECE = 1024
 F_PIECES = F // PIECE
 SLABS = D // P
-VECTOR_COLS = 512
+VECTOR_COLS = 576
 W_BUFS = 4
-X_MID_BUFS = 5
+X_AHEAD = 3
+X_MID_BUFS = 2 * X_AHEAD
 HID_BUFS = 6
 
 FLOPS = 2 * TOKENS * D * D + 2 * TOKENS * D * F
@@ -58,7 +59,7 @@ def tile_flashinferblock_pb_kernel(
 
         ident = const.tile([P, P], F32)
         make_identity(nc, ident[:])
-        neg_half = const.tile([P, GROUP], F32)
+        neg_half = const.tile([P, 1], F32)
         nc.vector.memset(neg_half[:], -0.5)
 
         gb_rows = const.tile([P, P], BF16)
@@ -72,20 +73,18 @@ def tile_flashinferblock_pb_kernel(
         gain_shift = const.tile([P, 2 * SLABS], F32)
         nc.vector.tensor_copy(out=gain_shift[:], in_=gb_ps[:, 0, 0 : 2 * SLABS])
 
-        b_proj_all = const.tile([P, D], BF16)
-        b_fc1_all = const.tile([P, F], BF16)
+        ident_bf16 = const.tile([P, P], BF16)
+        make_identity(nc, ident_bf16[:])
         ones = const.tile([P, P], BF16)
         nc.vector.memset(ones[:], 1.0)
-        bias_row = const.tile([P, PIECE], BF16)
-        nc.vector.memset(bias_row[:], 0.0)
+        b_proj_row = const.tile([P, D], BF16)
+        nc.vector.memset(b_proj_row[:], 0.0)
+        nc.sync.dma_start(out=b_proj_row[0:1, :], in_=b_proj.rearrange("(o n) -> o n", o=1))
+        b_fc1_all = const.tile([P, F], BF16)
 
-        def spread_bias(bias, spread):
-            nc.sync.dma_start(out=bias_row[0:1, :], in_=bias.rearrange("(o n) -> o n", o=1))
-            spread_ps = tp_psum.tile([P, PIECE], BF16, tag="tp")
-            for half in range(PIECE // BANK):
-                cols = slice(half * BANK, (half + 1) * BANK)
-                nc.tensor.matmul(out=spread_ps[:, cols], lhsT=ones[:], rhs=bias_row[:, cols], start=True, stop=True)
-            nc.scalar.copy(out=spread, in_=spread_ps[:])
+        def load_b_fc1(c):
+            cols = slice(c * PIECE, (c + 1) * PIECE)
+            nc.sync.dma_start(out=b_fc1_all[:, cols], in_=b_fc1[cols].partition_broadcast(P))
 
         wp_codes = keep.tile([P, PASSES, D], U32, align_bytes=64)
         wp_scales = keep.tile([P, PASSES, D], U8, align_bytes=64)
@@ -142,7 +141,7 @@ def tile_flashinferblock_pb_kernel(
             at_ps = tp_psum.tile([P, PASSES * 2, P], F32, tag="tp")
             for s in range(PASSES * 2):
                 nc.tensor.transpose(at_ps[:, s, :], words[:, s * P : (s + 1) * P], ident[:])
-            a_grouped = stage.tile([P, PASSES, P, PACK], BF16, align_bytes=64)
+            a_grouped = stage.tile([P, PASSES, P, PACK], BF16, align_bytes=64, bufs=3)
             nc.scalar.copy(
                 out=a_grouped[:].bitcast(F32),
                 in_=at_ps[:].rearrange("p (g u) r -> p g r u", u=2),
@@ -153,20 +152,19 @@ def tile_flashinferblock_pb_kernel(
 
         def add_bias_to_residual(x_raw):
             xm = rows.tile([P, D], F32, tag="x_mid", bufs=X_MID_BUFS, name="x_mid")
-            nc.gpsimd.tensor_tensor(out=xm[:], in0=x_raw[:], in1=b_proj_all[:], op=ALU.add)
+            for half in range(D // BANK):
+                cols = slice(half * BANK, (half + 1) * BANK)
+                xb_ps = acc_psum.tile([P, BANK], F32, tag="acc")
+                nc.tensor.matmul(out=xb_ps[:], lhsT=ident_bf16[:], rhs=x_raw[:, cols], start=True, stop=False)
+                nc.tensor.matmul(out=xb_ps[:], lhsT=ones[:], rhs=b_proj_row[:, cols], start=False, stop=True)
+                nc.scalar.copy(out=xm[:, cols], in_=xb_ps[:])
             return xm
 
-        def new_stats():
-            return {
-                "row_sum": rows.tile([P, 2 * GROUP], F32, tag="row_sum", bufs=2, name="row_sum"),
-                "neg_mean": rows.tile([P, GROUP], F32, tag="neg_mean", bufs=2, name="neg_mean"),
-                "sq_sum": rows.tile([P, GROUP], F32, tag="sq_sum", bufs=2, name="sq_sum"),
-                "var_eps": rows.tile([P, GROUP], F32, tag="var_eps", bufs=2, name="var_eps"),
-                "rstd": rows.tile([P, GROUP], F32, tag="rstd", bufs=2, name="rstd"),
-            }
+        squares = rows.tile([P, D], BF16, bufs=1)
 
-        def project(i, codes, scales, xm, stats):
+        def project_and_norm(i, codes, scales, xm):
             q = i % GROUP
+            row_sum = rows.tile([P, D // BANK], F32, tag="row_sum", name="row_sum")
             for half in range(D // BANK):
                 cols = slice(half * BANK, (half + 1) * BANK)
                 acc = acc_psum.tile([P, BANK], F32, tag="acc")
@@ -188,47 +186,33 @@ def tile_flashinferblock_pb_kernel(
                     in1=xm[:, cols],
                     op0=ALU.add,
                     op1=ALU.add,
-                    accum_out=stats["row_sum"][:, 2 * q + half : 2 * q + half + 1],
+                    accum_out=row_sum[:, half : half + 1],
                 )
             nc.sync.dma_start(out=x_mid_v[:, i, :], in_=xm[:])
+            neg_mean = rows.tile([P, 1], F32, tag="neg_mean", name="neg_mean")
             nc.vector.tensor_scalar(
-                out=stats["neg_mean"][:, q : q + 1],
-                in0=stats["row_sum"][:, 2 * q : 2 * q + 1],
-                scalar1=stats["row_sum"][:, 2 * q + 1 : 2 * q + 2],
+                out=neg_mean[:],
+                in0=row_sum[:, 0:1],
+                scalar1=row_sum[:, 1:2],
                 scalar2=-1.0 / D,
                 op0=ALU.add,
                 op1=ALU.mult,
             )
-            z = rows.tile([P, D], F32, tag="normed", name="normed")
+            sq_sum = rows.tile([P, 1], F32, tag="sq_sum", name="sq_sum")
             nc.scalar.activation(
-                out=z[:],
-                in_=xm[:],
-                func=ACT.Square,
-                bias=stats["neg_mean"][:, q : q + 1],
-                scale=1.0,
-                accum_out=stats["sq_sum"][:, q : q + 1],
+                out=squares[:], in_=xm[:], func=ACT.Square, bias=neg_mean[:], scale=1.0, accum_out=sq_sum[:]
+            )
+            var_eps = rows.tile([P, 1], F32, tag="var_eps", name="var_eps")
+            nc.gpsimd.tensor_scalar(
+                out=var_eps[:], in0=sq_sum[:], scalar1=1.0 / D, scalar2=EPS, op0=ALU.mult, op1=ALU.add
+            )
+            rstd = rows.tile([P, 1], F32, tag="rstd", name="rstd")
+            nc.gpsimd.tensor_tensor(out=rstd[:], in0=var_eps[:], in1=neg_half[:], op=ALU.pow)
+            z = rows.tile([P, D], F32, tag="normed", name="normed")
+            nc.vector.tensor_scalar(
+                out=z[:], in0=xm[:], scalar1=neg_mean[:], scalar2=rstd[:], op0=ALU.add, op1=ALU.mult
             )
             return z
-
-        def normalise(x_mid, normed, stats):
-            nc.vector.tensor_scalar(
-                out=stats["var_eps"][:],
-                in0=stats["sq_sum"][:],
-                scalar1=1.0 / D,
-                scalar2=EPS,
-                op0=ALU.mult,
-                op1=ALU.add,
-            )
-            nc.gpsimd.tensor_tensor(out=stats["rstd"][:], in0=stats["var_eps"][:], in1=neg_half[:], op=ALU.pow)
-            for q in range(GROUP):
-                nc.vector.tensor_scalar(
-                    out=normed[q][:],
-                    in0=x_mid[q][:],
-                    scalar1=stats["neg_mean"][:, q : q + 1],
-                    scalar2=stats["rstd"][:, q : q + 1],
-                    op0=ALU.add,
-                    op1=ALU.mult,
-                )
 
         def quantise_normed(normed, codes, scales):
             h_slabs = stage.tile([P, SLABS, GROUP * P], BF16, bufs=1)
@@ -243,20 +227,17 @@ def tile_flashinferblock_pb_kernel(
                     scale=gain_shift[:, j : j + 1],
                     bias=gain_shift[:, SLABS + j : SLABS + j + 1],
                 )
-            h_grouped = []
             for g in range(PASSES):
-                hg = stage.tile([P, GROUP * P, PACK], BF16, align_bytes=64, tag="h_grouped", name="h_grouped")
+                h_grouped = stage.tile([P, GROUP * P, PACK], BF16, align_bytes=64, bufs=1)
                 nc.vector.tensor_copy(
-                    out=hg[:].rearrange("p (c i) t -> p c t i", i=4),
+                    out=h_grouped[:].rearrange("p (c i) t -> p c t i", i=4),
                     in_=h_slabs[:, g * PACK : (g + 1) * PACK, :].rearrange("p t (c i) -> p c t i", i=4),
                 )
-                h_grouped.append(hg)
-            for g in range(PASSES):
                 toks = slice(g * GROUP * P, (g + 1) * GROUP * P)
                 nc.vector.quantize_mx(
                     out=codes[:, toks].bitcast(FP8X4),
                     scales=scales[:, toks],
-                    in_=h_grouped[g][:].rearrange("p r t -> p (r t)"),
+                    in_=h_grouped[:].rearrange("p r t -> p (r t)"),
                 )
 
         def mlp(c, i, codes, scales):
@@ -282,7 +263,6 @@ def tile_flashinferblock_pb_kernel(
             nc.scalar.activation(out=hid[:], in_=hid[:], func=ACT.Gelu)
             nc.sync.dma_start(out=hid_v[:, i, c * PIECE : (c + 1) * PIECE], in_=hid[:])
 
-        spread_bias(b_proj, b_proj_all[:])
         load_weight_piece(0)
         load_weight_piece(1)
         a_raw = [load_rows(attn_v, i, "a_raw") for i in range(GROUP)]
@@ -291,6 +271,7 @@ def tile_flashinferblock_pb_kernel(
         x_raw.extend([load_rows(x_v, i, "x_raw") for i in range(GROUP, TILES)])
         load_weight_piece(2)
         load_weight_piece(3)
+        load_b_fc1(0)
 
         quantise_weight_piece(0)
         quantise_weight_piece(1)
@@ -299,22 +280,20 @@ def tile_flashinferblock_pb_kernel(
             codes, scales = a_quant[i // GROUP]
             cols = slice((i % GROUP) * PASSES * P, (i % GROUP + 1) * PASSES * P)
             quantise_attention(a_raw[i], codes[:, cols], scales[:, cols])
-        x_mid = [add_bias_to_residual(x_raw[i]) for i in range(X_MID_BUFS)]
-        for c in range(F_PIECES):
-            spread_bias(b_fc1[c * PIECE : (c + 1) * PIECE], b_fc1_all[:, c * PIECE : (c + 1) * PIECE])
-
+        x_mid = [add_bias_to_residual(x_raw[i]) for i in range(X_AHEAD)]
         h_quant = []
-        for grp in range(GROUPS):
-            tiles = range(grp * GROUP, (grp + 1) * GROUP)
-            stats = new_stats()
-            codes, scales = a_quant[grp]
-            normed = [project(i, codes, scales, x_mid[i], stats) for i in tiles]
-            normalise([x_mid[i] for i in tiles], normed, stats)
-            if grp == 0:
-                x_mid.extend([add_bias_to_residual(x_raw[i]) for i in range(X_MID_BUFS, TILES)])
-            h_quant.append(token_codes())
-            quantise_normed(normed, h_quant[grp][0], h_quant[grp][1])
+        normed = []
+        for i in range(TILES):
+            if i + X_AHEAD < TILES:
+                x_mid.append(add_bias_to_residual(x_raw[i + X_AHEAD]))
+            codes, scales = a_quant[i // GROUP]
+            normed.append(project_and_norm(i, codes, scales, x_mid[i]))
+            if i % GROUP == GROUP - 1:
+                h_quant.append(token_codes())
+                quantise_normed(normed[i + 1 - GROUP : i + 1], h_quant[-1][0], h_quant[-1][1])
 
+        for c in range(1, F_PIECES):
+            load_b_fc1(c)
         for grp in range(GROUPS):
             for c in range(F_PIECES):
                 if grp == 0:

@@ -26,7 +26,7 @@ BANK = 512
 PIECE = 1024
 F_PIECES = F // PIECE
 SLABS = D // P
-VECTOR_COLS = 576
+VECTOR_COLS = 544
 W_BUFS = 4
 X_AHEAD = 3
 X_MID_BUFS = 2 * X_AHEAD
@@ -263,16 +263,18 @@ def tile_flashinferblock_pb_kernel(
             nc.scalar.activation(out=hid[:], in_=hid[:], func=ACT.Gelu)
             nc.sync.dma_start(out=hid_v[:, i, c * PIECE : (c + 1) * PIECE], in_=hid[:])
 
+        x_raw = [load_rows(x_v, i, "x_raw") for i in range(X_AHEAD)]
         load_weight_piece(0)
         load_weight_piece(1)
         a_raw = [load_rows(attn_v, i, "a_raw") for i in range(GROUP)]
-        x_raw = [load_rows(x_v, i, "x_raw") for i in range(GROUP)]
+        x_raw.extend([load_rows(x_v, i, "x_raw") for i in range(X_AHEAD, GROUP)])
         a_raw.extend([load_rows(attn_v, i, "a_raw") for i in range(GROUP, TILES)])
         x_raw.extend([load_rows(x_v, i, "x_raw") for i in range(GROUP, TILES)])
         load_weight_piece(2)
         load_weight_piece(3)
         load_b_fc1(0)
 
+        x_mid = [add_bias_to_residual(x_raw[i]) for i in range(X_AHEAD)]
         quantise_weight_piece(0)
         quantise_weight_piece(1)
         a_quant = [token_codes() for grp in range(GROUPS)]
@@ -280,7 +282,7 @@ def tile_flashinferblock_pb_kernel(
             codes, scales = a_quant[i // GROUP]
             cols = slice((i % GROUP) * PASSES * P, (i % GROUP + 1) * PASSES * P)
             quantise_attention(a_raw[i], codes[:, cols], scales[:, cols])
-        x_mid = [add_bias_to_residual(x_raw[i]) for i in range(X_AHEAD)]
+
         h_quant = []
         normed = []
         for i in range(TILES):
@@ -292,12 +294,16 @@ def tile_flashinferblock_pb_kernel(
                 h_quant.append(token_codes())
                 quantise_normed(normed[i + 1 - GROUP : i + 1], h_quant[-1][0], h_quant[-1][1])
 
+        def quantise_w_fc1_columns(c):
+            for g in range(PASSES):
+                quantise_weight_piece(PASSES + PASSES * c + g)
+
         for c in range(1, F_PIECES):
             load_b_fc1(c)
+        quantise_w_fc1_columns(0)
         for grp in range(GROUPS):
             for c in range(F_PIECES):
-                if grp == 0:
-                    for g in range(PASSES):
-                        quantise_weight_piece(PASSES + PASSES * c + g)
+                if grp == 0 and c + 1 < F_PIECES:
+                    quantise_w_fc1_columns(c + 1)
                 for i in range(grp * GROUP, (grp + 1) * GROUP):
                     mlp(c, i, h_quant[grp][0], h_quant[grp][1])

@@ -27,6 +27,8 @@ PIECE = 1024
 F_PIECES = F // PIECE
 SLABS = D // P
 VECTOR_COLS = 544
+GPSIMD_COLS = 768
+EARLY_PIECES = 4
 W_BUFS = 4
 X_AHEAD = 3
 X_MID_BUFS = 2 * X_AHEAD
@@ -112,11 +114,24 @@ def tile_flashinferblock_pb_kernel(
                 c, g = divmod(k - PASSES, PASSES)
                 cols = slice(c * PIECE, (c + 1) * PIECE)
                 codes, scales = wf_codes[:, g, cols], wf_scales[:, g, cols]
-            grouped = stage.tile([P, PIECE, PACK], BF16, align_bytes=64, tag="w_grouped", name="w_grouped")
             src = w_raw[k][:].rearrange("p t (c i) -> p c t i", i=4)
-            dst = grouped[:].rearrange("p (c i) t -> p c t i", i=4)
-            split = VECTOR_COLS // 4
-            nc.vector.tensor_copy(out=dst[:, 0:split], in_=src[:, 0:split])
+            if k < EARLY_PIECES:
+                grouped = stage.tile([P, PIECE, PACK], BF16, align_bytes=64, tag="w_grouped", name="w_grouped")
+                dst = grouped[:].rearrange("p (c i) t -> p c t i", i=4)
+                split = VECTOR_COLS // 4
+                nc.vector.tensor_copy(out=dst[:, 0:split], in_=src[:, 0:split])
+            else:
+                grouped = stage.tile([P, PIECE, PACK], BF16, align_bytes=64, tag="h_grouped", bufs=1, name="w_grouped_late")
+                dst = grouped[:].rearrange("p (c i) t -> p c t i", i=4)
+                split = GPSIMD_COLS // 4
+                nc.gpsimd.tensor_scalar(
+                    out=grouped[:, 0:GPSIMD_COLS, :],
+                    in0=w_raw[k][:, :, 0:GPSIMD_COLS].rearrange("p t n -> p n t"),
+                    scalar1=1.0,
+                    scalar2=0.0,
+                    op0=ALU.mult,
+                    op1=ALU.add,
+                )
             nc.scalar.copy(out=dst[:, split:], in_=src[:, split:])
             nc.vector.quantize_mx(
                 out=codes.bitcast(FP8X4),
@@ -160,8 +175,6 @@ def tile_flashinferblock_pb_kernel(
                 nc.scalar.copy(out=xm[:, cols], in_=xb_ps[:])
             return xm
 
-        squares = rows.tile([P, D], BF16, bufs=1)
-
         def project_and_norm(i, codes, scales, xm):
             q = i % GROUP
             row_sum = rows.tile([P, D // BANK], F32, tag="row_sum", name="row_sum")
@@ -199,8 +212,9 @@ def tile_flashinferblock_pb_kernel(
                 op1=ALU.mult,
             )
             sq_sum = rows.tile([P, 1], F32, tag="sq_sum", name="sq_sum")
+            z = rows.tile([P, D], F32, tag="normed", name="normed")
             nc.scalar.activation(
-                out=squares[:], in_=xm[:], func=ACT.Square, bias=neg_mean[:], scale=1.0, accum_out=sq_sum[:]
+                out=z[:], in_=xm[:], func=ACT.Square, bias=neg_mean[:], scale=1.0, accum_out=sq_sum[:]
             )
             var_eps = rows.tile([P, 1], F32, tag="var_eps", name="var_eps")
             nc.gpsimd.tensor_scalar(
@@ -208,7 +222,6 @@ def tile_flashinferblock_pb_kernel(
             )
             rstd = rows.tile([P, 1], F32, tag="rstd", name="rstd")
             nc.gpsimd.tensor_tensor(out=rstd[:], in0=var_eps[:], in1=neg_half[:], op=ALU.pow)
-            z = rows.tile([P, D], F32, tag="normed", name="normed")
             nc.vector.tensor_scalar(
                 out=z[:], in0=xm[:], scalar1=neg_mean[:], scalar2=rstd[:], op0=ALU.add, op1=ALU.mult
             )
@@ -228,7 +241,7 @@ def tile_flashinferblock_pb_kernel(
                     bias=gain_shift[:, SLABS + j : SLABS + j + 1],
                 )
             for g in range(PASSES):
-                h_grouped = stage.tile([P, GROUP * P, PACK], BF16, align_bytes=64, bufs=1)
+                h_grouped = stage.tile([P, GROUP * P, PACK], BF16, align_bytes=64, tag="h_grouped", bufs=1, name="h_grouped")
                 nc.vector.tensor_copy(
                     out=h_grouped[:].rearrange("p (c i) t -> p c t i", i=4),
                     in_=h_slabs[:, g * PACK : (g + 1) * PACK, :].rearrange("p t (c i) -> p c t i", i=4),
@@ -301,9 +314,8 @@ def tile_flashinferblock_pb_kernel(
         for c in range(1, F_PIECES):
             load_b_fc1(c)
         quantise_w_fc1_columns(0)
-        for grp in range(GROUPS):
-            for c in range(F_PIECES):
-                if grp == 0 and c + 1 < F_PIECES:
-                    quantise_w_fc1_columns(c + 1)
-                for i in range(grp * GROUP, (grp + 1) * GROUP):
-                    mlp(c, i, h_quant[grp][0], h_quant[grp][1])
+        for c in range(F_PIECES):
+            for i in range(TILES):
+                if c + 1 < F_PIECES and i % GROUP == 0:
+                    quantise_weight_piece(PASSES + PASSES * (c + 1) + i // GROUP)
+                mlp(c, i, h_quant[i // GROUP][0], h_quant[i // GROUP][1])

@@ -20,15 +20,15 @@ F = 4096
 EPS = 1e-5
 PASSES = D // K_PASS
 TILES = TOKENS // P
-GROUP = 4
+GROUP = 2
 GROUPS = TILES // GROUP
 BANK = 512
 PIECE = 1024
 F_PIECES = F // PIECE
 SLABS = D // P
 VECTOR_COLS = 544
-GPSIMD_COLS = 768
-EARLY_PIECES = 4
+GPSIMD_COLS = 1024
+EARLY_PIECES = 7
 W_BUFS = 4
 X_AHEAD = 3
 X_MID_BUFS = 2 * X_AHEAD
@@ -46,7 +46,7 @@ def tile_flashinferblock_pb_kernel(
         keep = ctx.enter_context(tc.tile_pool(name="keep", bufs=1))
         loads = ctx.enter_context(tc.tile_pool(name="loads", bufs=TILES))
         stage = ctx.enter_context(tc.tile_pool(name="stage", bufs=2))
-        rows = ctx.enter_context(tc.tile_pool(name="rows", bufs=GROUP))
+        rows = ctx.enter_context(tc.tile_pool(name="rows", bufs=4))
         tp_psum = ctx.enter_context(tc.psum_pool(name="tp_psum", bufs=3))
         acc_psum = ctx.enter_context(tc.psum_pool(name="acc_psum", bufs=5))
 
@@ -132,7 +132,8 @@ def tile_flashinferblock_pb_kernel(
                     op0=ALU.mult,
                     op1=ALU.add,
                 )
-            nc.scalar.copy(out=dst[:, split:], in_=src[:, split:])
+            if split < PIECE // 4:
+                nc.scalar.copy(out=dst[:, split:], in_=src[:, split:])
             nc.vector.quantize_mx(
                 out=codes.bitcast(FP8X4),
                 scales=scales,
@@ -228,7 +229,7 @@ def tile_flashinferblock_pb_kernel(
             return z
 
         def quantise_normed(normed, codes, scales):
-            h_slabs = stage.tile([P, SLABS, GROUP * P], BF16, bufs=1)
+            h_slabs = stage.tile([P, SLABS, GROUP * P], BF16, bufs=2)
             for j in range(SLABS):
                 zt_ps = tp_psum.tile([P, GROUP, P], F32, tag="tp")
                 for q in range(GROUP):
@@ -279,10 +280,10 @@ def tile_flashinferblock_pb_kernel(
         x_raw = [load_rows(x_v, i, "x_raw") for i in range(X_AHEAD)]
         load_weight_piece(0)
         load_weight_piece(1)
-        a_raw = [load_rows(attn_v, i, "a_raw") for i in range(GROUP)]
-        x_raw.extend([load_rows(x_v, i, "x_raw") for i in range(X_AHEAD, GROUP)])
-        a_raw.extend([load_rows(attn_v, i, "a_raw") for i in range(GROUP, TILES)])
-        x_raw.extend([load_rows(x_v, i, "x_raw") for i in range(GROUP, TILES)])
+        a_raw = [load_rows(attn_v, i, "a_raw") for i in range(TILES // 2)]
+        x_raw.extend([load_rows(x_v, i, "x_raw") for i in range(X_AHEAD, TILES // 2)])
+        a_raw.extend([load_rows(attn_v, i, "a_raw") for i in range(TILES // 2, TILES)])
+        x_raw.extend([load_rows(x_v, i, "x_raw") for i in range(TILES // 2, TILES)])
         load_weight_piece(2)
         load_weight_piece(3)
         load_b_fc1(0)
@@ -316,6 +317,6 @@ def tile_flashinferblock_pb_kernel(
         quantise_w_fc1_columns(0)
         for c in range(F_PIECES):
             for i in range(TILES):
-                if c + 1 < F_PIECES and i % GROUP == 0:
-                    quantise_weight_piece(PASSES + PASSES * (c + 1) + i // GROUP)
+                if c + 1 < F_PIECES and i % (TILES // PASSES) == 0:
+                    quantise_weight_piece(PASSES + PASSES * (c + 1) + i // (TILES // PASSES))
                 mlp(c, i, h_quant[i // GROUP][0], h_quant[i // GROUP][1])

@@ -176,7 +176,7 @@ def tile_flashinferblock_pb_kernel(
                 nc.scalar.copy(out=xm[:, cols], in_=xb_ps[:])
             return xm
 
-        def project_and_norm(i, codes, scales, xm):
+        def project_and_measure(i, codes, scales, xm):
             q = i % GROUP
             row_sum = rows.tile([P, D // BANK], F32, tag="row_sum", name="row_sum")
             for half in range(D // BANK):
@@ -223,6 +223,9 @@ def tile_flashinferblock_pb_kernel(
             )
             rstd = rows.tile([P, 1], F32, tag="rstd", name="rstd")
             nc.gpsimd.tensor_tensor(out=rstd[:], in0=var_eps[:], in1=neg_half[:], op=ALU.pow)
+            return z, neg_mean, rstd
+
+        def norm(xm, z, neg_mean, rstd):
             nc.vector.tensor_scalar(
                 out=z[:], in0=xm[:], scalar1=neg_mean[:], scalar2=rstd[:], op0=ALU.add, op1=ALU.mult
             )
@@ -299,14 +302,18 @@ def tile_flashinferblock_pb_kernel(
 
         h_quant = []
         normed = []
-        for i in range(TILES):
+        measured = []
+        for i in range(TILES + 1):
             if i + X_AHEAD < TILES:
                 x_mid.append(add_bias_to_residual(x_raw[i + X_AHEAD]))
-            codes, scales = a_quant[i // GROUP]
-            normed.append(project_and_norm(i, codes, scales, x_mid[i]))
-            if i % GROUP == GROUP - 1:
-                h_quant.append(token_codes())
-                quantise_normed(normed[i + 1 - GROUP : i + 1], h_quant[-1][0], h_quant[-1][1])
+            if i < TILES:
+                codes, scales = a_quant[i // GROUP]
+                measured.append(project_and_measure(i, codes, scales, x_mid[i]))
+            if i > 0:
+                normed.append(norm(x_mid[i - 1], measured[i - 1][0], measured[i - 1][1], measured[i - 1][2]))
+                if i % GROUP == 0:
+                    h_quant.append(token_codes())
+                    quantise_normed(normed[i - GROUP : i], h_quant[-1][0], h_quant[-1][1])
 
         def quantise_w_fc1_columns(c):
             for g in range(PASSES):

@@ -27,7 +27,8 @@ PIECE = 1024
 F_PIECES = F // PIECE
 SLABS = D // P
 VECTOR_COLS = 544
-GPSIMD_COLS = 1024
+LATE_SPAN = 5
+LATE_LEAD = 1
 EARLY_PIECES = 7
 W_BUFS = 4
 X_AHEAD = 3
@@ -107,33 +108,33 @@ def tile_flashinferblock_pb_kernel(
                 nc.sync.dma_start(out=raw[:], in_=wf_v[g][:, :, c * PIECE : (c + 1) * PIECE])
             w_raw[k] = raw
 
-        def quantise_weight_piece(k):
+        def regroup_weight_piece(k):
+            if k < EARLY_PIECES:
+                grouped = stage.tile([P, PIECE, PACK], BF16, align_bytes=64, tag="w_grouped", name="w_grouped")
+                src = w_raw[k][:].rearrange("p t (c i) -> p c t i", i=4)
+                dst = grouped[:].rearrange("p (c i) t -> p c t i", i=4)
+                split = VECTOR_COLS // 4
+                nc.vector.tensor_copy(out=dst[:, 0:split], in_=src[:, 0:split])
+                nc.scalar.copy(out=dst[:, split:], in_=src[:, split:])
+            else:
+                grouped = stage.tile([P, PIECE, PACK], BF16, align_bytes=64, tag="h_grouped", bufs=1, name="w_grouped_late")
+                nc.gpsimd.tensor_scalar(
+                    out=grouped[:],
+                    in0=w_raw[k][:].rearrange("p t n -> p n t"),
+                    scalar1=1.0,
+                    scalar2=0.0,
+                    op0=ALU.mult,
+                    op1=ALU.add,
+                )
+            return grouped
+
+        def quantise_grouped(k, grouped):
             if k < PASSES:
                 codes, scales = wp_codes[:, k, :], wp_scales[:, k, :]
             else:
                 c, g = divmod(k - PASSES, PASSES)
                 cols = slice(c * PIECE, (c + 1) * PIECE)
                 codes, scales = wf_codes[:, g, cols], wf_scales[:, g, cols]
-            src = w_raw[k][:].rearrange("p t (c i) -> p c t i", i=4)
-            if k < EARLY_PIECES:
-                grouped = stage.tile([P, PIECE, PACK], BF16, align_bytes=64, tag="w_grouped", name="w_grouped")
-                dst = grouped[:].rearrange("p (c i) t -> p c t i", i=4)
-                split = VECTOR_COLS // 4
-                nc.vector.tensor_copy(out=dst[:, 0:split], in_=src[:, 0:split])
-            else:
-                grouped = stage.tile([P, PIECE, PACK], BF16, align_bytes=64, tag="h_grouped", bufs=1, name="w_grouped_late")
-                dst = grouped[:].rearrange("p (c i) t -> p c t i", i=4)
-                split = GPSIMD_COLS // 4
-                nc.gpsimd.tensor_scalar(
-                    out=grouped[:, 0:GPSIMD_COLS, :],
-                    in0=w_raw[k][:, :, 0:GPSIMD_COLS].rearrange("p t n -> p n t"),
-                    scalar1=1.0,
-                    scalar2=0.0,
-                    op0=ALU.mult,
-                    op1=ALU.add,
-                )
-            if split < PIECE // 4:
-                nc.scalar.copy(out=dst[:, split:], in_=src[:, split:])
             nc.vector.quantize_mx(
                 out=codes.bitcast(FP8X4),
                 scales=scales,
@@ -141,6 +142,9 @@ def tile_flashinferblock_pb_kernel(
             )
             if k + W_BUFS < n_pieces:
                 load_weight_piece(k + W_BUFS)
+
+        def quantise_weight_piece(k):
+            quantise_grouped(k, regroup_weight_piece(k))
 
         def load_rows(view, i, tag):
             raw = loads.tile([P, D], BF16, tag=tag, name=tag)
@@ -176,7 +180,7 @@ def tile_flashinferblock_pb_kernel(
                 nc.scalar.copy(out=xm[:, cols], in_=xb_ps[:])
             return xm
 
-        def project_and_measure(i, codes, scales, xm):
+        def project(i, codes, scales, xm):
             q = i % GROUP
             row_sum = rows.tile([P, D // BANK], F32, tag="row_sum", name="row_sum")
             for half in range(D // BANK):
@@ -203,6 +207,9 @@ def tile_flashinferblock_pb_kernel(
                     accum_out=row_sum[:, half : half + 1],
                 )
             nc.sync.dma_start(out=x_mid_v[:, i, :], in_=xm[:])
+            return row_sum
+
+        def measure(xm, row_sum):
             neg_mean = rows.tile([P, 1], F32, tag="neg_mean", name="neg_mean")
             nc.vector.tensor_scalar(
                 out=neg_mean[:],
@@ -302,28 +309,36 @@ def tile_flashinferblock_pb_kernel(
 
         h_quant = []
         normed = []
+        row_sums = []
         measured = []
-        for i in range(TILES + 1):
+        for i in range(TILES + 2):
             if i + X_AHEAD < TILES:
                 x_mid.append(add_bias_to_residual(x_raw[i + X_AHEAD]))
             if i < TILES:
                 codes, scales = a_quant[i // GROUP]
-                measured.append(project_and_measure(i, codes, scales, x_mid[i]))
-            if i > 0:
-                normed.append(norm(x_mid[i - 1], measured[i - 1][0], measured[i - 1][1], measured[i - 1][2]))
-                if i % GROUP == 0:
+                row_sums.append(project(i, codes, scales, x_mid[i]))
+            if 0 < i <= TILES:
+                measured.append(measure(x_mid[i - 1], row_sums[i - 1]))
+            if i > 1:
+                normed.append(norm(x_mid[i - 2], measured[i - 2][0], measured[i - 2][1], measured[i - 2][2]))
+                if (i - 1) % GROUP == 0:
                     h_quant.append(token_codes())
-                    quantise_normed(normed[i - GROUP : i], h_quant[-1][0], h_quant[-1][1])
-
-        def quantise_w_fc1_columns(c):
-            for g in range(PASSES):
-                quantise_weight_piece(PASSES + PASSES * c + g)
+                    quantise_normed(normed[i - 1 - GROUP : i - 1], h_quant[-1][0], h_quant[-1][1])
 
         for c in range(1, F_PIECES):
             load_b_fc1(c)
-        quantise_w_fc1_columns(0)
+        for g in range(PASSES):
+            quantise_weight_piece(PASSES + g)
+        late = {}
         for c in range(F_PIECES):
             for i in range(TILES):
-                if c + 1 < F_PIECES and i % (TILES // PASSES) == 0:
-                    quantise_weight_piece(PASSES + PASSES * (c + 1) + i // (TILES // PASSES))
+                k = PASSES + PASSES * (c + 1) + i // (TILES // PASSES)
+                if i % (TILES // PASSES) == 0 and k < EARLY_PIECES:
+                    quantise_weight_piece(k)
+                for k in range(EARLY_PIECES, n_pieces + 1):
+                    if c * TILES + i == (F_PIECES - 1) * TILES - LATE_LEAD - LATE_SPAN * (n_pieces - k):
+                        if k > EARLY_PIECES:
+                            quantise_grouped(k - 1, late[k - 1])
+                        if k < n_pieces:
+                            late[k] = regroup_weight_piece(k)
                 mlp(c, i, h_quant[i // GROUP][0], h_quant[i // GROUP][1])

from contextlib import ExitStack

import concourse.mybir as mybir
from concourse.masks import make_identity

F32 = mybir.dt.float32
BF16 = mybir.dt.bfloat16
U32 = mybir.dt.uint32
U8 = mybir.dt.uint8
FP8X4 = mybir.dt.float8_e4m3fn_x4
ALU = mybir.AluOpType
ACT = mybir.ActivationFunctionType

P = 128
PACK = 4
K_PASS = P * PACK
TOKENS = 1024
D = 1024
F = 4096
EPS = 1e-5
PASSES = D // K_PASS
TILES = TOKENS // P
GROUP = 2
GROUPS = TILES // GROUP
BANK = 512
PIECE = 1024
F_PIECES = F // PIECE
SLABS = D // P
VECTOR_COLS = 544
LATE_SPAN = 5
LATE_LEAD = 1
EARLY_PIECES = 7
W_BUFS = 4
X_AHEAD = 3
X_MID_BUFS = 2 * X_AHEAD
HID_BUFS = 6

FLOPS = 2 * TOKENS * D * D + 2 * TOKENS * D * F


def tile_flashinferblock_pb_kernel(
    tc, attn_out, x, w_proj, b_proj, g2, beta2, w_fc1, b_fc1, out_0, out_1
):
    nc = tc.nc
    with ExitStack() as ctx:
        const = ctx.enter_context(tc.tile_pool(name="const", bufs=1))
        keep = ctx.enter_context(tc.tile_pool(name="keep", bufs=1))
        loads = ctx.enter_context(tc.tile_pool(name="loads", bufs=TILES))
        stage = ctx.enter_context(tc.tile_pool(name="stage", bufs=2))
        rows = ctx.enter_context(tc.tile_pool(name="rows", bufs=4))
        tp_psum = ctx.enter_context(tc.psum_pool(name="tp_psum", bufs=3))
        acc_psum = ctx.enter_context(tc.psum_pool(name="acc_psum", bufs=5))

        attn_v = attn_out.flatten_outer_dims().rearrange("(p i) k -> p i k", i=TILES)
        x_v = x.flatten_outer_dims().rearrange("(p i) d -> p i d", i=TILES)
        x_mid_v = out_0.flatten_outer_dims().rearrange("(p i) d -> p i d", i=TILES)
        hid_v = out_1.flatten_outer_dims().rearrange("(p i) f -> p i f", i=TILES)

        warm = const.tile([P, 1], F32)
        nc.vector.memset(warm[:], 0.0)
        nc.scalar.activation(out=warm[:], in_=warm[:], func=ACT.Gelu)

        ident = const.tile([P, P], F32)
        make_identity(nc, ident[:])
        neg_half = const.tile([P, 1], F32)
        nc.vector.memset(neg_half[:], -0.5)

        gb_rows = const.tile([P, P], BF16)
        nc.vector.memset(gb_rows[:], 0.0)
        nc.sync.dma_start(out=gb_rows[0:SLABS, :], in_=g2.rearrange("(j p) -> j p", p=P))
        nc.sync.dma_start(out=gb_rows[SLABS : 2 * SLABS, :], in_=beta2.rearrange("(j p) -> j p", p=P))
        gb_rows_f32 = const.tile([P, P], F32)
        nc.vector.tensor_copy(out=gb_rows_f32[:], in_=gb_rows[:])
        gb_ps = tp_psum.tile([P, GROUP, P], F32, tag="tp")
        nc.tensor.transpose(gb_ps[:, 0, :], gb_rows_f32[:], ident[:])
        gain_shift = const.tile([P, 2 * SLABS], F32)
        nc.vector.tensor_copy(out=gain_shift[:], in_=gb_ps[:, 0, 0 : 2 * SLABS])

        ident_bf16 = const.tile([P, P], BF16)
        make_identity(nc, ident_bf16[:])
        ones = const.tile([P, P], BF16)
        nc.vector.memset(ones[:], 1.0)
        b_proj_row = const.tile([P, D], BF16)
        nc.vector.memset(b_proj_row[:], 0.0)
        nc.sync.dma_start(out=b_proj_row[0:1, :], in_=b_proj.rearrange("(o n) -> o n", o=1))
        b_fc1_all = const.tile([P, F], BF16)

        def load_b_fc1(c):
            cols = slice(c * PIECE, (c + 1) * PIECE)
            nc.sync.dma_start(out=b_fc1_all[:, cols], in_=b_fc1[cols].partition_broadcast(P))

        wp_codes = keep.tile([P, PASSES, D], U32, align_bytes=64)
        wp_scales = keep.tile([P, PASSES, D], U8, align_bytes=64)
        wf_codes = keep.tile([P, PASSES, F], U32, align_bytes=64)
        wf_scales = keep.tile([P, PASSES, F], U8, align_bytes=64)

        wp_v = w_proj.rearrange("(g u p e) n -> g p u e n", g=PASSES, u=2, p=P, e=2)
        wf_v = w_fc1.rearrange("(g t p) n -> g p t n", g=PASSES, t=PACK, p=P)
        n_pieces = PASSES + PASSES * F_PIECES
        w_raw = {}

        def load_weight_piece(k):
            raw = loads.tile([P, PACK, PIECE], BF16, tag="w_raw", bufs=W_BUFS, name="w_raw")
            if k < PASSES:
                nc.sync.dma_start(out=raw[:].rearrange("p (u e) n -> p u e n", u=2), in_=wp_v[k])
            else:
                c, g = divmod(k - PASSES, PASSES)
                nc.sync.dma_start(out=raw[:], in_=wf_v[g][:, :, c * PIECE : (c + 1) * PIECE])
            w_raw[k] = raw

        def regroup_weight_piece(k):
            if k < EARLY_PIECES:
                grouped = stage.tile([P, PIECE, PACK], BF16, align_bytes=64, tag="w_grouped", name="w_grouped")
                src = w_raw[k][:].rearrange("p t (c i) -> p c t i", i=4)
                dst = grouped[:].rearrange("p (c i) t -> p c t i", i=4)
                split = VECTOR_COLS // 4
                nc.vector.tensor_copy(out=dst[:, 0:split], in_=src[:, 0:split])
                nc.scalar.copy(out=dst[:, split:], in_=src[:, split:])
            else:
                grouped = stage.tile([P, PIECE, PACK], BF16, align_bytes=64, tag="h_grouped", bufs=1, name="w_grouped_late")
                nc.gpsimd.tensor_scalar(
                    out=grouped[:],
                    in0=w_raw[k][:].rearrange("p t n -> p n t"),
                    scalar1=1.0,
                    scalar2=0.0,
                    op0=ALU.mult,
                    op1=ALU.add,
                )
            return grouped

        def quantise_grouped(k, grouped):
            if k < PASSES:
                codes, scales = wp_codes[:, k, :], wp_scales[:, k, :]
            else:
                c, g = divmod(k - PASSES, PASSES)
                cols = slice(c * PIECE, (c + 1) * PIECE)
                codes, scales = wf_codes[:, g, cols], wf_scales[:, g, cols]
            nc.vector.quantize_mx(
                out=codes.bitcast(FP8X4),
                scales=scales,
                in_=grouped[:].rearrange("p n t -> p (n t)"),
            )
            if k + W_BUFS < n_pieces:
                load_weight_piece(k + W_BUFS)

        def quantise_weight_piece(k):
            quantise_grouped(k, regroup_weight_piece(k))

        def load_rows(view, i, tag):
            raw = loads.tile([P, D], BF16, tag=tag, name=tag)
            nc.sync.dma_start(out=raw[:], in_=view[:, i, :])
            return raw

        def token_codes():
            codes = keep.tile([P, GROUP * PASSES * P], U32, align_bytes=64, tag="tok_codes", bufs=GROUPS, name="tok_codes")
            scales = keep.tile([P, GROUP * PASSES * P], U8, align_bytes=64, tag="tok_scales", bufs=GROUPS, name="tok_scales")
            return codes, scales

        def quantise_attention(a_raw, codes, scales):
            words = a_raw[:].bitcast(F32)
            at_ps = tp_psum.tile([P, PASSES * 2, P], F32, tag="tp")
            for s in range(PASSES * 2):
                nc.tensor.transpose(at_ps[:, s, :], words[:, s * P : (s + 1) * P], ident[:])
            a_grouped = stage.tile([P, PASSES, P, PACK], BF16, align_bytes=64, bufs=3)
            nc.scalar.copy(
                out=a_grouped[:].bitcast(F32),
                in_=at_ps[:].rearrange("p (g u) r -> p g r u", u=2),
            )
            nc.vector.quantize_mx(
                out=codes.bitcast(FP8X4), scales=scales, in_=a_grouped[:].rearrange("p g r t -> p (g r t)")
            )

        def add_bias_to_residual(x_raw):
            xm = rows.tile([P, D], F32, tag="x_mid", bufs=X_MID_BUFS, name="x_mid")
            for half in range(D // BANK):
                cols = slice(half * BANK, (half + 1) * BANK)
                xb_ps = acc_psum.tile([P, BANK], F32, tag="acc")
                nc.tensor.matmul(out=xb_ps[:], lhsT=ident_bf16[:], rhs=x_raw[:, cols], start=True, stop=False)
                nc.tensor.matmul(out=xb_ps[:], lhsT=ones[:], rhs=b_proj_row[:, cols], start=False, stop=True)
                nc.scalar.copy(out=xm[:, cols], in_=xb_ps[:])
            return xm

        def project(i, codes, scales, xm):
            q = i % GROUP
            row_sum = rows.tile([P, D // BANK], F32, tag="row_sum", name="row_sum")
            for half in range(D // BANK):
                cols = slice(half * BANK, (half + 1) * BANK)
                acc = acc_psum.tile([P, BANK], F32, tag="acc")
                for g in range(PASSES):
                    toks = slice((q * PASSES + g) * P, (q * PASSES + g + 1) * P)
                    nc.tensor.matmul_mx(
                        out=acc[:],
                        lhsT=codes[:, toks].bitcast(FP8X4),
                        lhsT_scale=scales[:, toks],
                        rhs=wp_codes[:, g, cols].bitcast(FP8X4),
                        rhs_scale=wp_scales[:, g, cols],
                        start=(g == 0),
                        stop=(g == PASSES - 1),
                    )
                nc.vector.scalar_tensor_tensor(
                    out=xm[:, cols],
                    in0=acc[:],
                    scalar=0.0,
                    in1=xm[:, cols],
                    op0=ALU.add,
                    op1=ALU.add,
                    accum_out=row_sum[:, half : half + 1],
                )
            nc.sync.dma_start(out=x_mid_v[:, i, :], in_=xm[:])
            return row_sum

        def measure(xm, row_sum):
            neg_mean = rows.tile([P, 1], F32, tag="neg_mean", name="neg_mean")
            nc.vector.tensor_scalar(
                out=neg_mean[:],
                in0=row_sum[:, 0:1],
                scalar1=row_sum[:, 1:2],
                scalar2=-1.0 / D,
                op0=ALU.add,
                op1=ALU.mult,
            )
            sq_sum = rows.tile([P, 1], F32, tag="sq_sum", name="sq_sum")
            z = rows.tile([P, D], F32, tag="normed", name="normed")
            nc.scalar.activation(
                out=z[:], in_=xm[:], func=ACT.Square, bias=neg_mean[:], scale=1.0, accum_out=sq_sum[:]
            )
            var_eps = rows.tile([P, 1], F32, tag="var_eps", name="var_eps")
            nc.gpsimd.tensor_scalar(
                out=var_eps[:], in0=sq_sum[:], scalar1=1.0 / D, scalar2=EPS, op0=ALU.mult, op1=ALU.add
            )
            rstd = rows.tile([P, 1], F32, tag="rstd", name="rstd")
            nc.gpsimd.tensor_tensor(out=rstd[:], in0=var_eps[:], in1=neg_half[:], op=ALU.pow)
            return z, neg_mean, rstd

        def norm(xm, z, neg_mean, rstd):
            nc.vector.tensor_scalar(
                out=z[:], in0=xm[:], scalar1=neg_mean[:], scalar2=rstd[:], op0=ALU.add, op1=ALU.mult
            )
            return z

        def quantise_normed(normed, codes, scales):
            h_slabs = stage.tile([P, SLABS, GROUP * P], BF16, bufs=2)
            for j in range(SLABS):
                zt_ps = tp_psum.tile([P, GROUP, P], F32, tag="tp")
                for q in range(GROUP):
                    nc.tensor.transpose(zt_ps[:, q, :], normed[q][:, j * P : (j + 1) * P], ident[:])
                nc.scalar.activation(
                    out=h_slabs[:, j, :],
                    in_=zt_ps[:].rearrange("p q r -> p (q r)"),
                    func=ACT.Identity,
                    scale=gain_shift[:, j : j + 1],
                    bias=gain_shift[:, SLABS + j : SLABS + j + 1],
                )
            for g in range(PASSES):
                h_grouped = stage.tile([P, GROUP * P, PACK], BF16, align_bytes=64, tag="h_grouped", bufs=1, name="h_grouped")
                nc.vector.tensor_copy(
                    out=h_grouped[:].rearrange("p (c i) t -> p c t i", i=4),
                    in_=h_slabs[:, g * PACK : (g + 1) * PACK, :].rearrange("p t (c i) -> p c t i", i=4),
                )
                toks = slice(g * GROUP * P, (g + 1) * GROUP * P)
                nc.vector.quantize_mx(
                    out=codes[:, toks].bitcast(FP8X4),
                    scales=scales[:, toks],
                    in_=h_grouped[:].rearrange("p r t -> p (r t)"),
                )

        def mlp(c, i, codes, scales):
            q = i % GROUP
            hid = rows.tile([P, PIECE], F32, tag="hid", bufs=HID_BUFS, name="hid")
            for half in range(PIECE // BANK):
                cols = slice(c * PIECE + half * BANK, c * PIECE + (half + 1) * BANK)
                acc = acc_psum.tile([P, BANK], F32, tag="acc")
                for g in range(PASSES):
                    toks = slice((g * GROUP + q) * P, (g * GROUP + q + 1) * P)
                    nc.tensor.matmul_mx(
                        out=acc[:],
                        lhsT=codes[:, toks].bitcast(FP8X4),
                        lhsT_scale=scales[:, toks],
                        rhs=wf_codes[:, g, cols].bitcast(FP8X4),
                        rhs_scale=wf_scales[:, g, cols],
                        start=(g == 0),
                        stop=(g == PASSES - 1),
                    )
                nc.vector.tensor_tensor(
                    out=hid[:, half * BANK : (half + 1) * BANK], in0=acc[:], in1=b_fc1_all[:, cols], op=ALU.add
                )
            nc.scalar.activation(out=hid[:], in_=hid[:], func=ACT.Gelu)
            nc.sync.dma_start(out=hid_v[:, i, c * PIECE : (c + 1) * PIECE], in_=hid[:])

        x_raw = [load_rows(x_v, i, "x_raw") for i in range(X_AHEAD)]
        load_weight_piece(0)
        load_weight_piece(1)
        a_raw = [load_rows(attn_v, i, "a_raw") for i in range(TILES // 2)]
        x_raw.extend([load_rows(x_v, i, "x_raw") for i in range(X_AHEAD, TILES // 2)])
        a_raw.extend([load_rows(attn_v, i, "a_raw") for i in range(TILES // 2, TILES)])
        x_raw.extend([load_rows(x_v, i, "x_raw") for i in range(TILES // 2, TILES)])
        load_weight_piece(2)
        load_weight_piece(3)
        load_b_fc1(0)

        x_mid = [add_bias_to_residual(x_raw[i]) for i in range(X_AHEAD)]
        quantise_weight_piece(0)
        quantise_weight_piece(1)
        a_quant = [token_codes() for grp in range(GROUPS)]
        for i in range(TILES):
            codes, scales = a_quant[i // GROUP]
            cols = slice((i % GROUP) * PASSES * P, (i % GROUP + 1) * PASSES * P)
            quantise_attention(a_raw[i], codes[:, cols], scales[:, cols])

        h_quant = []
        normed = []
        row_sums = []
        measured = []
        for i in range(TILES + 2):
            if i + X_AHEAD < TILES:
                x_mid.append(add_bias_to_residual(x_raw[i + X_AHEAD]))
            if i < TILES:
                codes, scales = a_quant[i // GROUP]
                row_sums.append(project(i, codes, scales, x_mid[i]))
            if 0 < i <= TILES:
                measured.append(measure(x_mid[i - 1], row_sums[i - 1]))
            if i > 1:
                normed.append(norm(x_mid[i - 2], measured[i - 2][0], measured[i - 2][1], measured[i - 2][2]))
                if (i - 1) % GROUP == 0:
                    h_quant.append(token_codes())
                    quantise_normed(normed[i - 1 - GROUP : i - 1], h_quant[-1][0], h_quant[-1][1])

        for c in range(1, F_PIECES):
            load_b_fc1(c)
        for g in range(PASSES):
            quantise_weight_piece(PASSES + g)
        late = {}
        for c in range(F_PIECES):
            for i in range(TILES):
                k = PASSES + PASSES * (c + 1) + i // (TILES // PASSES)
                if i % (TILES // PASSES) == 0 and k < EARLY_PIECES:
                    quantise_weight_piece(k)
                for k in range(EARLY_PIECES, n_pieces + 1):
                    if c * TILES + i == (F_PIECES - 1) * TILES - LATE_LEAD - LATE_SPAN * (n_pieces - k):
                        if k > EARLY_PIECES:
                            quantise_grouped(k - 1, late[k - 1])
                        if k < n_pieces:
                            late[k] = regroup_weight_piece(k)
                mlp(c, i, h_quant[i // GROUP][0], h_quant[i // GROUP][1])
